import numpy as np
import ml_dtypes


def mxq(x, axis, fmt="e4m3"):
    dtype, down = {"e4m3": (ml_dtypes.float8_e4m3fn, 7), "e5m2": (ml_dtypes.float8_e5m2, 14)}[fmt]
    v = np.moveaxis(np.asarray(x, np.float32).astype(ml_dtypes.bfloat16).astype(np.float64), axis, -1)
    blocks = v.reshape(v.shape[:-1] + (-1, 32))
    amax = np.abs(blocks).max(-1, keepdims=True)
    byte = np.maximum(np.where(amax > 0, np.frexp(amax)[1] - 1 + 127, 0) - down, 1)
    scale = np.exp2(byte - 127.0)
    codes = (blocks / scale).astype(np.float32).astype(dtype).astype(np.float64)
    return np.moveaxis((codes * scale).reshape(v.shape), -1, axis)


WIDE = False


def mx_kscale(k):
    if not WIDE:
        return np.ones(k)
    levels = np.array([10, -10, 5, -5, 0])
    a = np.random.permutation(np.resize(levels, k // 512 * 4)).reshape(k // 512, 4)
    idx = np.arange(k)
    return np.exp2(a[idx // 512, idx % 128 // 32])


BF16 = ml_dtypes.bfloat16


def bf(x):
    return np.asarray(x, np.float32).astype(BF16)


def f64(x):
    return np.asarray(x).astype(np.float64)


E2M1 = np.array([0.0, 0.5, 1.0, 1.5, 2.0, 3.0, 4.0, 6.0, -0.0, -0.5, -1.0, -1.5, -2.0, -3.0, -4.0, -6.0])


def pack_weight(w, fmt):
    k, n = w.shape
    w = f64(bf(w)).reshape(k // 32, 32, n)
    amax = np.abs(w).max(1)
    if fmt == "e4m3":
        byte = np.frexp(amax)[1] - 1 + 127 - 7
    else:
        mant, ex = np.frexp(amax / 6.0)
        byte = np.where(mant > 0.5, ex, ex - 1) + 127
    byte = np.clip(np.where(amax > 0, byte, 1), 1, 254)
    scaled = (w * np.exp2(127.0 - byte)[:, None, :]).reshape(k, n).astype(np.float32)
    by_word = np.ascontiguousarray(scaled.reshape(k // 512, 128, 4, n).transpose(0, 1, 3, 2))
    if fmt == "e4m3":
        words = by_word.astype(ml_dtypes.float8_e4m3fn).view(np.uint8)
    else:
        c = by_word.astype(ml_dtypes.float4_e2m1fn).view(np.uint8) & 0xF
        words = c[..., 0::2] | (c[..., 1::2] << 4)
    return np.ascontiguousarray(words), np.ascontiguousarray(byte.astype(np.uint8).reshape(k // 512, 16, n))


def unpack_weight(words, scales, fmt):
    g, p, n, _ = words.shape
    if fmt == "e4m3":
        vals = np.ascontiguousarray(words).view(ml_dtypes.float8_e4m3fn).astype(np.float64)
    else:
        nib = np.empty((g, p, n, 4), np.uint8)
        nib[..., 0::2] = words & 0xF
        nib[..., 1::2] = words >> 4
        vals = E2M1[nib]
    vals = vals * np.repeat(np.exp2(scales.astype(np.float64) - 127.0), 8, axis=1)[..., None]
    return vals.transpose(0, 1, 3, 2).reshape(g * 512, n)

def pack4(w):
    words, scales = pack_weight(w, "e2m1")
    return words.reshape(words.shape[0], 128, -1), scales


def unpack4(words, scales):
    return unpack_weight(words.reshape(words.shape[0], 128, -1, 2), scales, "e2m1")


B, G, DB, DR = 128, 4, 512, 1024


def mish(v):
    return v * np.tanh(np.log(1.0 + np.exp(v)))


def setup_inputs():
    s, t = mx_kscale(DR), mx_kscale(DB)
    BB_feature = bf(np.random.standard_normal((B, G, DB)) * t)
    RF_feature = bf(np.random.standard_normal((B, DR)) * s)
    W_bbbb = np.random.standard_normal((DB, DB)) / np.sqrt(DB) / t
    b_bbbb = bf(np.random.standard_normal(DB) * 0.5)
    W_rfbb = np.random.standard_normal((DB, DR)) / np.sqrt(DR) / s
    b_rfbb = bf(np.random.standard_normal(DB) * 0.5)
    W_bbbb_words, W_bbbb_scales = pack4(np.ascontiguousarray(W_bbbb.T))
    W_rfbb_words, W_rfbb_scales = pack4(np.ascontiguousarray(W_rfbb.T))
    return {"BB_feature": BB_feature,
            "RF_feature": RF_feature,
            "W_bbbb_words": W_bbbb_words,
            "W_bbbb_scales": W_bbbb_scales,
            "b_bbbb": b_bbbb,
            "W_rfbb_words": W_rfbb_words,
            "W_rfbb_scales": W_rfbb_scales,
            "b_rfbb": b_rfbb}


def reference(BB_feature, RF_feature, W_bbbb_words, W_bbbb_scales, b_bbbb, W_rfbb_words, W_rfbb_scales, b_rfbb):
    RF_to_BB = mish((mxq(f64(RF_feature), 1, "e4m3") @ unpack4(W_rfbb_words, W_rfbb_scales)) + f64(b_rfbb))
    BB_to_BB = mish((mxq(f64(BB_feature), 2, "e4m3") @ unpack4(W_bbbb_words, W_bbbb_scales)) + f64(b_bbbb))
    return BB_to_BB + RF_to_BB[:, None, :]

@@ -1,0 +1,161 @@
+import concourse.mybir as mybir
+from concourse.masks import make_identity
+
+F32 = mybir.dt.float32
+BF16 = mybir.dt.bfloat16
+I32 = mybir.dt.int32
+U32 = mybir.dt.uint32
+U8 = mybir.dt.uint8
+FP8X4 = mybir.dt.float8_e4m3fn_x4
+FP4X4 = mybir.dt.float4_e2m1fn_x4
+ACT = mybir.ActivationFunctionType
+ALU = mybir.AluOpType
+
+P = 128
+GROUPS = 4
+N_OUT = 512
+K_PASS = 512
+WORDS = K_PASS // 2
+RF = GROUPS
+
+FLOPS = 2 * P * 1024 * N_OUT + 2 * P * GROUPS * 512 * N_OUT
+
+
+def load_weight(nc, keep, words, scales, name):
+    passes = words.shape[0]
+    codes = keep.tile([P, passes, 2 * N_OUT], U8, name=name + "_codes", align_bytes=64)
+    plane = keep.tile([P, passes, N_OUT], U8, name=name + "_plane", align_bytes=64)
+    nc.vector.memset(plane[:].bitcast(I32), 0)
+    nc.sync.dma_start(out=codes[:].bitcast(I32), in_=words.bitcast(I32).rearrange("g p c -> p g c"))
+    for quadrant in range(4):
+        nc.sync.dma_start(
+            out=plane[32 * quadrant : 32 * quadrant + 4, :, :].bitcast(I32),
+            in_=scales.bitcast(I32)[:, 4 * quadrant : 4 * quadrant + 4, :].rearrange("g r c -> r g c"),
+        )
+    return codes, plane
+
+
+def tile_gnn_layer_pb_s_kernel(
+    tc, BB_feature, RF_feature, W_bbbb_words, W_bbbb_scales, b_bbbb, W_rfbb_words, W_rfbb_scales, b_rfbb, out
+):
+    nc = tc.nc
+    features = [
+        BB_feature[:, 0:2, :],
+        BB_feature[:, 2:4, :],
+        RF_feature.rearrange("b (s k) -> b s k", s=2),
+    ]
+    with (
+        tc.tile_pool(name="keep", bufs=1) as keep,
+        tc.tile_pool(name="feat", bufs=len(features)) as feat,
+        tc.tile_pool(name="work", bufs=GROUPS + 1) as work,
+        tc.psum_pool(name="psum_t", bufs=2) as psum_t,
+        tc.psum_pool(name="psum_acc", bufs=6) as psum_acc,
+        tc.manual_schedule(),
+    ):
+        bias_rows = keep.tile([P, 2, N_OUT], BF16)
+        nc.vector.memset(bias_rows[:].bitcast(I32), 0)
+        ones = keep.tile([P, P], BF16)
+        nc.vector.memset(ones[:], 1.0)
+        zero_column = keep.tile([P, 1], F32)
+        nc.vector.memset(zero_column[:], 0.0)
+        first_table = keep.tile([P, 1], F32)
+        nc.scalar.activation(out=first_table[:], in_=zero_column[:], func=ACT.Sigmoid)
+        identity = keep.tile([P, P], F32)
+        make_identity(nc, identity[:])
+
+        nc.sync.dma_start(out=bias_rows[0:1, 0, :], in_=b_bbbb.unsqueeze(0))
+        nc.sync.dma_start(out=bias_rows[0:1, 1, :], in_=b_rfbb.unsqueeze(0))
+        x_tiles = []
+        for source in features:
+            x = feat.tile([P, 2, K_PASS], BF16)
+            nc.sync.dma_start(out=x[:], in_=source)
+            x_tiles.append(x)
+        bb_codes, bb_plane = load_weight(nc, keep, W_bbbb_words, W_bbbb_scales, "w_bb")
+        rf_codes, rf_plane = load_weight(nc, keep, W_rfbb_words, W_rfbb_scales, "w_rf")
+
+        biases = []
+        for i in range(2):
+            bias_psum = psum_acc.tile([P, N_OUT], F32, tag="acc")
+            nc.tensor.matmul(out=bias_psum[:], lhsT=ones[:], rhs=bias_rows[:, i, :], start=True, stop=True)
+            bias = keep.tile([P, N_OUT], F32, name="bias%d" % i)
+            nc.scalar.copy(out=bias[:], in_=bias_psum[:])
+            biases.append(bias)
+
+        x_codes = []
+        x_planes = []
+        for x in x_tiles:
+            x_words = x[:].bitcast(F32)
+            transposed = psum_t.tile([P, 2, 2, P], F32)
+            for s in range(2):
+                for u in range(2):
+                    nc.tensor.transpose(transposed[:, s, u, :], x_words[:, s, u:WORDS:2], identity[:])
+            grouped = feat.tile([P, 2 * P * 4], BF16, align_bytes=64)
+            nc.scalar.copy(
+                out=grouped[:].bitcast(F32).rearrange("p (s b u) -> p s b u", s=2, u=2),
+                in_=transposed[:].rearrange("p s u b -> p s b u"),
+            )
+            codes = feat.tile([P, 2 * P], U32, align_bytes=64)
+            plane = feat.tile([P, 2 * P], U8, align_bytes=64)
+            nc.vector.quantize_mx(out=codes[:].bitcast(FP8X4), scales=plane[:], in_=grouped[:])
+            x_codes.append(codes)
+            x_planes.append(plane)
+
+        def mx_pass(acc, pass_index, w_codes, w_plane, start, stop):
+            tile_index, half = divmod(pass_index, 2)
+            samples = slice(half * P, (half + 1) * P)
+            nc.tensor.matmul_mx(
+                out=acc[:],
+                lhsT=x_codes[tile_index][:, samples].bitcast(FP8X4),
+                lhsT_scale=x_planes[tile_index][:, samples],
+                rhs=w_codes.bitcast(FP4X4),
+                rhs_scale=w_plane,
+                start=start,
+                stop=stop,
+            )
+
+        products = []
+        for g in range(GROUPS):
+            acc = psum_acc.tile([P, N_OUT], F32, tag="acc")
+            mx_pass(acc, g, bb_codes[:, 0, :], bb_plane[:, 0, :], True, True)
+            products.append(acc)
+        acc = psum_acc.tile([P, N_OUT], F32, tag="acc")
+        for s in range(2):
+            mx_pass(acc, GROUPS + s, rf_codes[:, s, :], rf_plane[:, s, :], s == 0, s == 1)
+        products.append(acc)
+
+        v_tiles = []
+        q_tiles = []
+        q2_tiles = []
+
+        def square_q(i):
+            q2 = work.tile([P, N_OUT], F32)
+            nc.vector.tensor_tensor(out=q2[:], in0=q_tiles[i][:], in1=q_tiles[i][:], op=ALU.mult)
+            q2_tiles.append(q2)
+
+        for i in range(GROUPS + 1):
+            v = work.tile([P, N_OUT], F32)
+            nc.vector.tensor_tensor(out=v[:], in0=products[i][:], in1=biases[i // GROUPS][:], op=ALU.add)
+            q = work.tile([P, N_OUT], F32)
+            nc.scalar.activation(out=q[:], in_=v[:], func=ACT.Sigmoid, scale=-1.0)
+            v_tiles.append(v)
+            q_tiles.append(q)
+            if i > 0:
+                square_q(i - 1)
+        square_q(GROUPS)
+
+        mish_rf = None
+        for i in [RF] + list(range(GROUPS)):
+            root = work.tile([P, N_OUT], F32)
+            nc.scalar.activation(out=root[:], in_=q2_tiles[i][:], func=ACT.Abs_reciprocal_sqrt, scale=0.5, bias=0.5)
+            ratio = work.tile([P, N_OUT], F32)
+            nc.scalar.activation(out=ratio[:], in_=root[:], func=ACT.Square)
+            mish = work.tile([P, N_OUT], F32)
+            nc.vector.scalar_tensor_tensor(
+                out=mish[:], in0=ratio[:], scalar=-1.0, in1=v_tiles[i][:], op0=ALU.add, op1=ALU.mult
+            )
+            if i == RF:
+                mish_rf = mish
+            else:
+                total = work.tile([P, N_OUT], F32)
+                nc.vector.tensor_tensor(out=total[:], in0=mish[:], in1=mish_rf[:], op=ALU.add)
+                nc.sync.dma_start(out=out[:, i, :], in_=total[:])

@@ -52,34 +52,26 @@ def tile_gnn_layer_pb_s_kernel(
         tc.psum_pool(name="psum_acc", bufs=6) as psum_acc,
         tc.manual_schedule(),
     ):
+        x_tiles = []
+        for source in features:
+            x = feat.tile([P, 2, K_PASS], BF16)
+            nc.sync.dma_start(out=x[:], in_=source)
+            x_tiles.append(x)
         bias_rows = keep.tile([P, 2, N_OUT], BF16)
         nc.vector.memset(bias_rows[:].bitcast(I32), 0)
+        nc.scalar.dma_start(out=bias_rows[0:1, 0, :], in_=b_bbbb.unsqueeze(0))
+        nc.scalar.dma_start(out=bias_rows[0:1, 1, :], in_=b_rfbb.unsqueeze(0))
+        bb_codes, bb_plane = load_weight(nc, keep, W_bbbb_words, W_bbbb_scales, "w_bb")
+        rf_codes, rf_plane = load_weight(nc, keep, W_rfbb_words, W_rfbb_scales, "w_rf")
+
+        identity = keep.tile([P, P], F32)
+        make_identity(nc, identity[:])
         ones = keep.tile([P, P], BF16)
         nc.vector.memset(ones[:], 1.0)
         zero_column = keep.tile([P, 1], F32)
         nc.vector.memset(zero_column[:], 0.0)
         first_table = keep.tile([P, 1], F32)
         nc.scalar.activation(out=first_table[:], in_=zero_column[:], func=ACT.Sigmoid)
-        identity = keep.tile([P, P], F32)
-        make_identity(nc, identity[:])
-
-        nc.sync.dma_start(out=bias_rows[0:1, 0, :], in_=b_bbbb.unsqueeze(0))
-        nc.sync.dma_start(out=bias_rows[0:1, 1, :], in_=b_rfbb.unsqueeze(0))
-        x_tiles = []
-        for source in features:
-            x = feat.tile([P, 2, K_PASS], BF16)
-            nc.sync.dma_start(out=x[:], in_=source)
-            x_tiles.append(x)
-        bb_codes, bb_plane = load_weight(nc, keep, W_bbbb_words, W_bbbb_scales, "w_bb")
-        rf_codes, rf_plane = load_weight(nc, keep, W_rfbb_words, W_rfbb_scales, "w_rf")
-
-        biases = []
-        for i in range(2):
-            bias_psum = psum_acc.tile([P, N_OUT], F32, tag="acc")
-            nc.tensor.matmul(out=bias_psum[:], lhsT=ones[:], rhs=bias_rows[:, i, :], start=True, stop=True)
-            bias = keep.tile([P, N_OUT], F32, name="bias%d" % i)
-            nc.scalar.copy(out=bias[:], in_=bias_psum[:])
-            biases.append(bias)
 
         x_codes = []
         x_planes = []
@@ -99,6 +91,14 @@ def tile_gnn_layer_pb_s_kernel(
             nc.vector.quantize_mx(out=codes[:].bitcast(FP8X4), scales=plane[:], in_=grouped[:])
             x_codes.append(codes)
             x_planes.append(plane)
+
+        biases = []
+        for i in range(2):
+            bias_psum = psum_acc.tile([P, N_OUT], F32, tag="acc")
+            nc.tensor.matmul(out=bias_psum[:], lhsT=ones[:], rhs=bias_rows[:, i, :], start=True, stop=True)
+            bias = keep.tile([P, N_OUT], F32, name="bias%d" % i)
+            nc.scalar.copy(out=bias[:], in_=bias_psum[:])
+            biases.append(bias)
 
         def mx_pass(acc, pass_index, w_codes, w_plane, start, stop):
             tile_index, half = divmod(pass_index, 2)
@@ -125,13 +125,6 @@ def tile_gnn_layer_pb_s_kernel(
 
         v_tiles = []
         q_tiles = []
-        q2_tiles = []
-
-        def square_q(i):
-            q2 = work.tile([P, N_OUT], F32)
-            nc.vector.tensor_tensor(out=q2[:], in0=q_tiles[i][:], in1=q_tiles[i][:], op=ALU.mult)
-            q2_tiles.append(q2)
-
         for i in range(GROUPS + 1):
             v = work.tile([P, N_OUT], F32)
             nc.vector.tensor_tensor(out=v[:], in0=products[i][:], in1=biases[i // GROUPS][:], op=ALU.add)
@@ -139,23 +132,40 @@ def tile_gnn_layer_pb_s_kernel(
             nc.scalar.activation(out=q[:], in_=v[:], func=ACT.Sigmoid, scale=-1.0)
             v_tiles.append(v)
             q_tiles.append(q)
-            if i > 0:
-                square_q(i - 1)
-        square_q(GROUPS)
 
-        mish_rf = None
-        for i in [RF] + list(range(GROUPS)):
+        rf_first = [RF] + list(range(GROUPS))
+        q2_tiles = {}
+        for i in rf_first:
+            q2 = work.tile([P, N_OUT], F32)
+            nc.vector.tensor_tensor(out=q2[:], in0=q_tiles[i][:], in1=q_tiles[i][:], op=ALU.mult)
+            q2_tiles[i] = q2
+        roots = {}
+        mishes = {}
+
+        def take_root(i):
             root = work.tile([P, N_OUT], F32)
             nc.scalar.activation(out=root[:], in_=q2_tiles[i][:], func=ACT.Abs_reciprocal_sqrt, scale=0.5, bias=0.5)
+            roots[i] = root
+
+        def square_and_multiply(i):
             ratio = work.tile([P, N_OUT], F32)
-            nc.scalar.activation(out=ratio[:], in_=root[:], func=ACT.Square)
+            nc.scalar.activation(out=ratio[:], in_=roots[i][:], func=ACT.Square)
             mish = work.tile([P, N_OUT], F32)
             nc.vector.scalar_tensor_tensor(
                 out=mish[:], in0=ratio[:], scalar=-1.0, in1=v_tiles[i][:], op0=ALU.add, op1=ALU.mult
             )
-            if i == RF:
-                mish_rf = mish
-            else:
-                total = work.tile([P, N_OUT], F32)
-                nc.vector.tensor_tensor(out=total[:], in0=mish[:], in1=mish_rf[:], op=ALU.add)
-                nc.sync.dma_start(out=out[:, i, :], in_=total[:])
+            mishes[i] = mish
+
+        def sum_and_store(g):
+            total = work.tile([P, N_OUT], F32)
+            nc.vector.tensor_tensor(out=total[:], in0=mishes[g][:], in1=mishes[RF][:], op=ALU.add)
+            nc.sync.dma_start(out=out[:, g, :], in_=total[:])
+
+        count = len(rf_first)
+        for step in range(count + 2):
+            if step < count:
+                take_root(rf_first[step])
+            if 0 <= step - 1 < count:
+                square_and_multiply(rf_first[step - 1])
+            if 1 <= step - 2 < count:
+                sum_and_store(rf_first[step - 2])

@@ -149,7 +149,10 @@ def tile_gnn_layer_pb_s_kernel(
 
         def square_and_multiply(i):
             ratio = work.tile([P, N_OUT], F32)
-            nc.scalar.activation(out=ratio[:], in_=roots[i][:], func=ACT.Square)
+            if i == RF:
+                nc.vector.tensor_tensor(out=ratio[:], in0=roots[i][:], in1=roots[i][:], op=ALU.mult)
+            else:
+                nc.scalar.activation(out=ratio[:], in_=roots[i][:], func=ACT.Square)
             mish = work.tile([P, N_OUT], F32)
             nc.vector.scalar_tensor_tensor(
                 out=mish[:], in0=ratio[:], scalar=-1.0, in1=v_tiles[i][:], op0=ALU.add, op1=ALU.mult

@@ -18,6 +18,10 @@ K_PASS = 512
 WORDS = K_PASS // 2
 RF = GROUPS
 
+LOAD_ORDER = (0, 2, 1)
+FIRST_HALF = "T0 C0 Q0 T2 C2 Q2 T1 C1 M0 M1 A0 Q1 M4 M2 M3 G0 A1 G1 A4 G4 A2 G2 A3 G3"
+SECOND_HALF = "Wv4 Wv0 Pv4 Pv0 Wv1 Rs4 Rs0 Rs1 Wv2 Xv4 Rs2 Ss1 Xv0 Wv3 Ss2 Xv1 Yv0 Rs3 Xv2 Yv1 Ss3 Xv3 Yv2 Yv3"
+
 FLOPS = 2 * P * 1024 * N_OUT + 2 * P * GROUPS * 512 * N_OUT
 
 
@@ -48,57 +52,68 @@ def tile_gnn_layer_pb_s_kernel(
         tc.tile_pool(name="keep", bufs=1) as keep,
         tc.tile_pool(name="feat", bufs=len(features)) as feat,
         tc.tile_pool(name="work", bufs=GROUPS + 1) as work,
-        tc.psum_pool(name="psum_t", bufs=2) as psum_t,
-        tc.psum_pool(name="psum_acc", bufs=6) as psum_acc,
+        tc.psum_pool(name="psum_t", bufs=3) as psum_t,
+        tc.psum_pool(name="psum_acc", bufs=5) as psum_acc,
         tc.manual_schedule(),
     ):
-        x_tiles = []
-        for source in features:
-            x = feat.tile([P, 2, K_PASS], BF16)
-            nc.sync.dma_start(out=x[:], in_=source)
-            x_tiles.append(x)
-        bias_rows = keep.tile([P, 2, N_OUT], BF16)
-        nc.vector.memset(bias_rows[:].bitcast(I32), 0)
-        nc.scalar.dma_start(out=bias_rows[0:1, 0, :], in_=b_bbbb.unsqueeze(0))
-        nc.scalar.dma_start(out=bias_rows[0:1, 1, :], in_=b_rfbb.unsqueeze(0))
+        x_tiles = {}
+
+        def load_features(i, queue):
+            x = feat.tile([P, 2, K_PASS], BF16, name="x")
+            queue.dma_start(out=x[:], in_=features[i])
+            x_tiles[i] = x
+
+        biases = []
+
+        def load_bias(vec, queue):
+            bias = keep.tile([P, N_OUT], BF16, name="bias%d" % len(biases))
+            queue.dma_start(out=bias[:], in_=vec.partition_broadcast(P))
+            biases.append(bias)
+
+        load_bias(b_bbbb, nc.scalar)
+        load_bias(b_rfbb, nc.scalar)
+        for i in LOAD_ORDER:
+            load_features(i, nc.sync)
         bb_codes, bb_plane = load_weight(nc, keep, W_bbbb_words, W_bbbb_scales, "w_bb")
         rf_codes, rf_plane = load_weight(nc, keep, W_rfbb_words, W_rfbb_scales, "w_rf")
 
         identity = keep.tile([P, P], F32)
         make_identity(nc, identity[:])
-        ones = keep.tile([P, P], BF16)
-        nc.vector.memset(ones[:], 1.0)
         zero_column = keep.tile([P, 1], F32)
         nc.vector.memset(zero_column[:], 0.0)
         first_table = keep.tile([P, 1], F32)
         nc.scalar.activation(out=first_table[:], in_=zero_column[:], func=ACT.Sigmoid)
 
-        x_codes = []
-        x_planes = []
-        for x in x_tiles:
-            x_words = x[:].bitcast(F32)
-            transposed = psum_t.tile([P, 2, 2, P], F32)
+        transposed_tiles = {}
+        grouped_tiles = {}
+        x_codes = {}
+        x_planes = {}
+        products = {}
+        v_tiles = {}
+        q_tiles = {}
+
+        def transpose(i):
+            x_words = x_tiles[i][:].bitcast(F32)
+            transposed = psum_t.tile([P, 2, 2, P], F32, name="transposed")
             for s in range(2):
                 for u in range(2):
                     nc.tensor.transpose(transposed[:, s, u, :], x_words[:, s, u:WORDS:2], identity[:])
-            grouped = feat.tile([P, 2 * P * 4], BF16, align_bytes=64)
+            transposed_tiles[i] = transposed
+
+        def regroup(i):
+            grouped = feat.tile([P, 2 * P * 4], BF16, align_bytes=64, name="grouped")
             nc.scalar.copy(
                 out=grouped[:].bitcast(F32).rearrange("p (s b u) -> p s b u", s=2, u=2),
-                in_=transposed[:].rearrange("p s u b -> p s b u"),
+                in_=transposed_tiles[i][:].rearrange("p s u b -> p s b u"),
             )
-            codes = feat.tile([P, 2 * P], U32, align_bytes=64)
-            plane = feat.tile([P, 2 * P], U8, align_bytes=64)
-            nc.vector.quantize_mx(out=codes[:].bitcast(FP8X4), scales=plane[:], in_=grouped[:])
-            x_codes.append(codes)
-            x_planes.append(plane)
+            grouped_tiles[i] = grouped
 
-        biases = []
-        for i in range(2):
-            bias_psum = psum_acc.tile([P, N_OUT], F32, tag="acc")
-            nc.tensor.matmul(out=bias_psum[:], lhsT=ones[:], rhs=bias_rows[:, i, :], start=True, stop=True)
-            bias = keep.tile([P, N_OUT], F32, name="bias%d" % i)
-            nc.scalar.copy(out=bias[:], in_=bias_psum[:])
-            biases.append(bias)
+        def quantise(i):
+            codes = feat.tile([P, 2 * P], U32, align_bytes=64, name="codes")
+            plane = feat.tile([P, 2 * P], U8, align_bytes=64, name="plane")
+            nc.vector.quantize_mx(out=codes[:].bitcast(FP8X4), scales=plane[:], in_=grouped_tiles[i][:])
+            x_codes[i] = codes
+            x_planes[i] = plane
 
         def mx_pass(acc, pass_index, w_codes, w_plane, start, stop):
             tile_index, half = divmod(pass_index, 2)
@@ -113,62 +128,85 @@ def tile_gnn_layer_pb_s_kernel(
                 stop=stop,
             )
 
-        products = []
-        for g in range(GROUPS):
-            acc = psum_acc.tile([P, N_OUT], F32, tag="acc")
-            mx_pass(acc, g, bb_codes[:, 0, :], bb_plane[:, 0, :], True, True)
-            products.append(acc)
-        acc = psum_acc.tile([P, N_OUT], F32, tag="acc")
-        for s in range(2):
-            mx_pass(acc, GROUPS + s, rf_codes[:, s, :], rf_plane[:, s, :], s == 0, s == 1)
-        products.append(acc)
+        def multiply(i):
+            acc = psum_acc.tile([P, N_OUT], F32, name="acc")
+            if i == RF:
+                for s in range(2):
+                    mx_pass(acc, GROUPS + s, rf_codes[:, s, :], rf_plane[:, s, :], s == 0, s == 1)
+            else:
+                mx_pass(acc, i, bb_codes[:, 0, :], bb_plane[:, 0, :], True, True)
+            products[i] = acc
 
-        v_tiles = []
-        q_tiles = []
-        for i in range(GROUPS + 1):
-            v = work.tile([P, N_OUT], F32)
+        def add_bias(i):
+            v = work.tile([P, N_OUT], F32, name="v")
             nc.vector.tensor_tensor(out=v[:], in0=products[i][:], in1=biases[i // GROUPS][:], op=ALU.add)
-            q = work.tile([P, N_OUT], F32)
-            nc.scalar.activation(out=q[:], in_=v[:], func=ACT.Sigmoid, scale=-1.0)
-            v_tiles.append(v)
-            q_tiles.append(q)
+            v_tiles[i] = v
 
-        rf_first = [RF] + list(range(GROUPS))
-        q2_tiles = {}
-        for i in rf_first:
-            q2 = work.tile([P, N_OUT], F32)
-            nc.vector.tensor_tensor(out=q2[:], in0=q_tiles[i][:], in1=q_tiles[i][:], op=ALU.mult)
-            q2_tiles[i] = q2
+        def sigmoid(i):
+            q = work.tile([P, N_OUT], F32, name="q")
+            nc.scalar.activation(out=q[:], in_=v_tiles[i][:], func=ACT.Sigmoid, scale=-1.0)
+            q_tiles[i] = q
+
+        steps = {"T": transpose, "C": regroup, "Q": quantise, "M": multiply, "A": add_bias, "G": sigmoid}
+        for word in FIRST_HALF.split():
+            steps[word[0]](int(word[1]))
+
+        engines = {"v": nc.vector, "s": nc.scalar, "g": nc.gpsimd}
+        w_tiles = {}
+        d_tiles = {}
         roots = {}
+        ratios = {}
         mishes = {}
 
-        def take_root(i):
-            root = work.tile([P, N_OUT], F32)
-            nc.scalar.activation(out=root[:], in_=q2_tiles[i][:], func=ACT.Abs_reciprocal_sqrt, scale=0.5, bias=0.5)
-            roots[i] = root
-
-        def square_and_multiply(i):
-            ratio = work.tile([P, N_OUT], F32)
-            if i == RF:
-                nc.vector.tensor_tensor(out=ratio[:], in0=roots[i][:], in1=roots[i][:], op=ALU.mult)
+        def square_q(e, i):
+            w = work.tile([P, N_OUT], F32, name="w")
+            if e == "s":
+                nc.scalar.activation(out=w[:], in_=q_tiles[i][:], func=ACT.Square)
             else:
-                nc.scalar.activation(out=ratio[:], in_=roots[i][:], func=ACT.Square)
-            mish = work.tile([P, N_OUT], F32)
+                engines[e].tensor_tensor(out=w[:], in0=q_tiles[i][:], in1=q_tiles[i][:], op=ALU.mult)
+            w_tiles[i] = w
+
+        def square_ahead(e, i):
+            d = work.tile([P, N_OUT], F32, name="d")
             nc.vector.scalar_tensor_tensor(
-                out=mish[:], in0=ratio[:], scalar=-1.0, in1=v_tiles[i][:], op0=ALU.add, op1=ALU.mult
+                out=d[:], in0=w_tiles[i][:], scalar=2.0, in1=w_tiles[i][:], op0=ALU.add, op1=ALU.mult
+            )
+            d_tiles[i] = d
+
+        def take_root(e, i):
+            if i in d_tiles:
+                ratio = work.tile([P, N_OUT], F32, name="ratio")
+                nc.scalar.activation(
+                    out=ratio[:], in_=d_tiles[i][:], func=ACT.Abs_reciprocal_sqrt, scale=0.25, bias=0.25
+                )
+                ratios[i] = ratio
+            else:
+                root = work.tile([P, N_OUT], F32, name="root")
+                nc.scalar.activation(
+                    out=root[:], in_=w_tiles[i][:], func=ACT.Abs_reciprocal_sqrt, scale=0.5, bias=0.5
+                )
+                roots[i] = root
+
+        def square_root(e, i):
+            ratio = work.tile([P, N_OUT], F32, name="ratio")
+            if e == "s":
+                nc.scalar.activation(out=ratio[:], in_=roots[i][:], func=ACT.Square)
+            else:
+                engines[e].tensor_tensor(out=ratio[:], in0=roots[i][:], in1=roots[i][:], op=ALU.mult)
+            ratios[i] = ratio
+
+        def multiply_v(e, i):
+            mish = work.tile([P, N_OUT], F32, name="mish")
+            nc.vector.scalar_tensor_tensor(
+                out=mish[:], in0=ratios[i][:], scalar=-1.0, in1=v_tiles[i][:], op0=ALU.add, op1=ALU.mult
             )
             mishes[i] = mish
 
-        def sum_and_store(g):
-            total = work.tile([P, N_OUT], F32)
-            nc.vector.tensor_tensor(out=total[:], in0=mishes[g][:], in1=mishes[RF][:], op=ALU.add)
+        def sum_and_store(e, g):
+            total = work.tile([P, N_OUT], F32, name="total")
+            engines[e].tensor_tensor(out=total[:], in0=mishes[g][:], in1=mishes[RF][:], op=ALU.add)
             nc.sync.dma_start(out=out[:, g, :], in_=total[:])
 
-        count = len(rf_first)
-        for step in range(count + 2):
-            if step < count:
-                take_root(rf_first[step])
-            if 0 <= step - 1 < count:
-                square_and_multiply(rf_first[step - 1])
-            if 1 <= step - 2 < count:
-                sum_and_store(rf_first[step - 2])
+        steps2 = {"W": square_q, "P": square_ahead, "R": take_root, "S": square_root, "X": multiply_v, "Y": sum_and_store}
+        for word in SECOND_HALF.split():
+            steps2[word[0]](word[1], int(word[2]))

@@ -19,7 +19,7 @@ WORDS = K_PASS // 2
 RF = GROUPS
 
 LOAD_ORDER = (0, 2, 1)
-FIRST_HALF = "T0 C0 Q0 T2 C2 Q2 T1 C1 M0 M1 A0 Q1 M4 M2 M3 G0 A1 G1 A4 G4 A2 G2 A3 G3"
+FIRST_HALF = "T0 C0 Q0 T2 C2 B0 K0 Q2 T1 C1 M0 M1 B1 A0 Q1 K1 M4 M2 M3 G0 A1 G1 A4 G4 A2 G2 A3 G3"
 SECOND_HALF = "Wv4 Wv0 Pv4 Pv0 Wv1 Rs4 Rs0 Rs1 Wv2 Xv4 Rs2 Ss1 Xv0 Wv3 Ss2 Xv1 Yv0 Rs3 Xv2 Yv1 Ss3 Xv3 Yv2 Yv3"
 
 FLOPS = 2 * P * 1024 * N_OUT + 2 * P * GROUPS * 512 * N_OUT
@@ -52,7 +52,8 @@ def tile_gnn_layer_pb_s_kernel(
         tc.tile_pool(name="keep", bufs=1) as keep,
         tc.tile_pool(name="feat", bufs=len(features)) as feat,
         tc.tile_pool(name="work", bufs=GROUPS + 1) as work,
-        tc.psum_pool(name="psum_t", bufs=3) as psum_t,
+        tc.psum_pool(name="psum_t", bufs=2) as psum_t,
+        tc.psum_pool(name="psum_b", bufs=1) as psum_b,
         tc.psum_pool(name="psum_acc", bufs=5) as psum_acc,
         tc.manual_schedule(),
     ):
@@ -63,15 +64,14 @@ def tile_gnn_layer_pb_s_kernel(
             queue.dma_start(out=x[:], in_=features[i])
             x_tiles[i] = x
 
-        biases = []
+        biases = {}
 
-        def load_bias(vec, queue):
-            bias = keep.tile([P, N_OUT], BF16, name="bias%d" % len(biases))
-            queue.dma_start(out=bias[:], in_=vec.partition_broadcast(P))
-            biases.append(bias)
-
-        load_bias(b_bbbb, nc.scalar)
-        load_bias(b_rfbb, nc.scalar)
+        bias_rows = keep.tile([P, 2, N_OUT], BF16)
+        nc.vector.memset(bias_rows[:].bitcast(I32), 0)
+        nc.scalar.dma_start(out=bias_rows[0:1, 0, :], in_=b_bbbb.unsqueeze(0))
+        nc.scalar.dma_start(out=bias_rows[0:1, 1, :], in_=b_rfbb.unsqueeze(0))
+        ones = keep.tile([P, P], BF16)
+        nc.vector.memset(ones[:], 1.0)
         for i in LOAD_ORDER:
             load_features(i, nc.sync)
         bb_codes, bb_plane = load_weight(nc, keep, W_bbbb_words, W_bbbb_scales, "w_bb")
@@ -137,6 +137,18 @@ def tile_gnn_layer_pb_s_kernel(
                 mx_pass(acc, i, bb_codes[:, 0, :], bb_plane[:, 0, :], True, True)
             products[i] = acc
 
+        bias_banks = {}
+
+        def spread_bias(i):
+            bank = psum_b.tile([P, N_OUT], F32, name="bias_bank")
+            nc.tensor.matmul(out=bank[:], lhsT=ones[:], rhs=bias_rows[:, i, :], start=True, stop=True)
+            bias_banks[i] = bank
+
+        def keep_bias(i):
+            bias = keep.tile([P, N_OUT], F32, name="bias%d" % i)
+            nc.scalar.copy(out=bias[:], in_=bias_banks[i][:])
+            biases[i] = bias
+
         def add_bias(i):
             v = work.tile([P, N_OUT], F32, name="v")
             nc.vector.tensor_tensor(out=v[:], in0=products[i][:], in1=biases[i // GROUPS][:], op=ALU.add)
@@ -147,7 +159,7 @@ def tile_gnn_layer_pb_s_kernel(
             nc.scalar.activation(out=q[:], in_=v_tiles[i][:], func=ACT.Sigmoid, scale=-1.0)
             q_tiles[i] = q
 
-        steps = {"T": transpose, "C": regroup, "Q": quantise, "M": multiply, "A": add_bias, "G": sigmoid}
+        steps = {"T": transpose, "C": regroup, "Q": quantise, "M": multiply, "A": add_bias, "G": sigmoid, "B": spread_bias, "K": keep_bias}
         for word in FIRST_HALF.split():
             steps[word[0]](int(word[1]))
 

@@ -19,8 +19,8 @@ WORDS = K_PASS // 2
 RF = GROUPS
 
 LOAD_ORDER = (0, 2, 1)
-FIRST_HALF = "T0 C0 Q0 T2 C2 B0 K0 Q2 T1 C1 M0 M1 B1 A0 Q1 K1 M4 M2 M3 G0 A1 G1 A4 G4 A2 G2 A3 G3"
-SECOND_HALF = "Wv4 Wv0 Pv4 Pv0 Wv1 Rs4 Rs0 Rs1 Wv2 Xv4 Rs2 Ss1 Xv0 Wv3 Ss2 Xv1 Yv0 Rs3 Xv2 Yv1 Ss3 Xv3 Yv2 Yv3"
+FIRST_HALF = "T0 C0 Q0 T2 C2 B0 K0 Q2 T1 C1 M0 M1 B1 A0 Q1 K1 M4 M2 M3 G0 Wg0 A1 G1 A4 G4 A2 G2 A3 G3"
+SECOND_HALF = "Wv4 Wv1 Pv4 Pv0 Wv2 Pv1 Rs4 Rs0 Rs1 Wv3 Xv4 Rs2 Xv0 Rs3 Ss2 Xv1 Yv0 Ss3 Xv2 Yv1 Xv3 Yv2 Yv3"
 
 FLOPS = 2 * P * 1024 * N_OUT + 2 * P * GROUPS * 512 * N_OUT
 
@@ -160,8 +160,6 @@ def tile_gnn_layer_pb_s_kernel(
             q_tiles[i] = q
 
         steps = {"T": transpose, "C": regroup, "Q": quantise, "M": multiply, "A": add_bias, "G": sigmoid, "B": spread_bias, "K": keep_bias}
-        for word in FIRST_HALF.split():
-            steps[word[0]](int(word[1]))
 
         engines = {"v": nc.vector, "s": nc.scalar, "g": nc.gpsimd}
         w_tiles = {}
@@ -219,6 +217,16 @@ def tile_gnn_layer_pb_s_kernel(
             engines[e].tensor_tensor(out=total[:], in0=mishes[g][:], in1=mishes[RF][:], op=ALU.add)
             nc.sync.dma_start(out=out[:, g, :], in_=total[:])
 
-        steps2 = {"W": square_q, "P": square_ahead, "R": take_root, "S": square_root, "X": multiply_v, "Y": sum_and_store}
-        for word in SECOND_HALF.split():
-            steps2[word[0]](word[1], int(word[2]))
+        def sum_and_store_halves(e, g):
+            total = work.tile([P, N_OUT], F32, name="total")
+            for half, queue in enumerate((nc.sync, nc.scalar)):
+                cols = slice(half * (N_OUT // 2), (half + 1) * (N_OUT // 2))
+                engines[e].tensor_tensor(out=total[:, cols], in0=mishes[g][:, cols], in1=mishes[RF][:, cols], op=ALU.add)
+                queue.dma_start(out=out[:, g, cols], in_=total[:, cols])
+
+        steps2 = {"Z": sum_and_store_halves, "W": square_q, "P": square_ahead, "R": take_root, "S": square_root, "X": multiply_v, "Y": sum_and_store}
+        for word in (FIRST_HALF + " " + SECOND_HALF).split():
+            if len(word) == 2:
+                steps[word[0]](int(word[1]))
+            else:
+                steps2[word[0]](word[1], int(word[2]))

@@ -19,8 +19,8 @@ WORDS = K_PASS // 2
 RF = GROUPS
 
 LOAD_ORDER = (0, 2, 1)
-FIRST_HALF = "T0 C0 Q0 T2 C2 B0 K0 Q2 T1 C1 M0 M1 B1 A0 Q1 K1 M4 M2 M3 G0 Wg0 A1 G1 A4 G4 A2 G2 A3 G3"
-SECOND_HALF = "Wv4 Wv1 Pv4 Pv0 Wv2 Pv1 Rs4 Rs0 Rs1 Wv3 Xv4 Rs2 Xv0 Rs3 Ss2 Xv1 Yv0 Ss3 Xv2 Yv1 Xv3 Yv2 Yv3"
+FIRST_HALF = "T0 C0 Q0 T2 C2 B0 K0 Q2 T1 C1 M0 M1 B1 A0 Q1 K1 M4 M2 M3 G0 Wg0 A1 G1 A4 G4 Ws1 A2 G2 A3 G3"
+SECOND_HALF = "Wv4 Pv0 Pv4 Wv2 Pv1 Wv3 Rs4 Rs0 Rs1 Rs2 Xv4 Rs3 Xv0 Ss2 Xv1 Yv0 Ss3 Yv1 Xv2 Xv3 Yv2 Yv3"
 
 FLOPS = 2 * P * 1024 * N_OUT + 2 * P * GROUPS * 512 * N_OUT
 
@@ -140,12 +140,12 @@ def tile_gnn_layer_pb_s_kernel(
         bias_banks = {}
 
         def spread_bias(i):
-            bank = psum_b.tile([P, N_OUT], F32, name="bias_bank")
+            bank = psum_b.tile([P, N_OUT], BF16, name="bias_bank")
             nc.tensor.matmul(out=bank[:], lhsT=ones[:], rhs=bias_rows[:, i, :], start=True, stop=True)
             bias_banks[i] = bank
 
         def keep_bias(i):
-            bias = keep.tile([P, N_OUT], F32, name="bias%d" % i)
+            bias = keep.tile([P, N_OUT], BF16, name="bias%d" % i)
             nc.scalar.copy(out=bias[:], in_=bias_banks[i][:])
             biases[i] = bias
 

@@ -19,7 +19,7 @@ WORDS = K_PASS // 2
 RF = GROUPS
 
 LOAD_ORDER = (0, 2, 1)
-FIRST_HALF = "T0 C0 Q0 T2 C2 B0 K0 Q2 T1 C1 M0 M1 B1 A0 Q1 K1 M4 M2 M3 G0 Wg0 A1 G1 A4 G4 Ws1 A2 G2 A3 G3"
+FIRST_HALF = "T0 C0 Q0 T2 C2 B0 B1 K0 Q2 T1 C1 M0 M1 A0 Q1 K1 M4 M2 M3 G0 Wg0 A1 G1 A4 G4 Ws1 A2 G2 A3 G3"
 SECOND_HALF = "Wv4 Pv0 Pv4 Wv2 Pv1 Wv3 Rs4 Rs0 Rs1 Rs2 Xv4 Rs3 Xv0 Ss2 Xv1 Yv0 Ss3 Yv1 Xv2 Xv3 Yv2 Yv3"
 
 FLOPS = 2 * P * 1024 * N_OUT + 2 * P * GROUPS * 512 * N_OUT
@@ -140,13 +140,14 @@ def tile_gnn_layer_pb_s_kernel(
         bias_banks = {}
 
         def spread_bias(i):
-            bank = psum_b.tile([P, N_OUT], BF16, name="bias_bank")
-            nc.tensor.matmul(out=bank[:], lhsT=ones[:], rhs=bias_rows[:, i, :], start=True, stop=True)
-            bias_banks[i] = bank
+            if "both" not in bias_banks:
+                bank = psum_b.tile([P, 2, N_OUT], BF16, name="bias_bank")
+                bias_banks["both"] = bank
+            nc.tensor.matmul(out=bias_banks["both"][:, i, :], lhsT=ones[:], rhs=bias_rows[:, i, :], start=True, stop=True)
 
         def keep_bias(i):
             bias = keep.tile([P, N_OUT], BF16, name="bias%d" % i)
-            nc.scalar.copy(out=bias[:], in_=bias_banks[i][:])
+            nc.scalar.copy(out=bias[:], in_=bias_banks["both"][:, i, :])
             biases[i] = bias
 
         def add_bias(i):

import concourse.mybir as mybir
from concourse.masks import make_identity

F32 = mybir.dt.float32
BF16 = mybir.dt.bfloat16
I32 = mybir.dt.int32
U32 = mybir.dt.uint32
U8 = mybir.dt.uint8
FP8X4 = mybir.dt.float8_e4m3fn_x4
FP4X4 = mybir.dt.float4_e2m1fn_x4
ACT = mybir.ActivationFunctionType
ALU = mybir.AluOpType

P = 128
GROUPS = 4
N_OUT = 512
K_PASS = 512
WORDS = K_PASS // 2
RF = GROUPS

LOAD_ORDER = (0, 2, 1)
FIRST_HALF = "T0 C0 Q0 T2 C2 B0 B1 K0 Q2 T1 C1 M0 M1 A0 Q1 K1 M4 M2 M3 G0 Wg0 A1 G1 A4 G4 Ws1 A2 G2 A3 G3"
SECOND_HALF = "Wv4 Pv0 Pv4 Wv2 Pv1 Wv3 Rs4 Rs0 Rs1 Rs2 Xv4 Rs3 Xv0 Ss2 Xv1 Yv0 Ss3 Yv1 Xv2 Xv3 Yv2 Yv3"

FLOPS = 2 * P * 1024 * N_OUT + 2 * P * GROUPS * 512 * N_OUT


def load_weight(nc, keep, words, scales, name):
    passes = words.shape[0]
    codes = keep.tile([P, passes, 2 * N_OUT], U8, name=name + "_codes", align_bytes=64)
    plane = keep.tile([P, passes, N_OUT], U8, name=name + "_plane", align_bytes=64)
    nc.vector.memset(plane[:].bitcast(I32), 0)
    nc.sync.dma_start(out=codes[:].bitcast(I32), in_=words.bitcast(I32).rearrange("g p c -> p g c"))
    for quadrant in range(4):
        nc.sync.dma_start(
            out=plane[32 * quadrant : 32 * quadrant + 4, :, :].bitcast(I32),
            in_=scales.bitcast(I32)[:, 4 * quadrant : 4 * quadrant + 4, :].rearrange("g r c -> r g c"),
        )
    return codes, plane


def tile_gnn_layer_pb_s_kernel(
    tc, BB_feature, RF_feature, W_bbbb_words, W_bbbb_scales, b_bbbb, W_rfbb_words, W_rfbb_scales, b_rfbb, out
):
    nc = tc.nc
    features = [
        BB_feature[:, 0:2, :],
        BB_feature[:, 2:4, :],
        RF_feature.rearrange("b (s k) -> b s k", s=2),
    ]
    with (
        tc.tile_pool(name="keep", bufs=1) as keep,
        tc.tile_pool(name="feat", bufs=len(features)) as feat,
        tc.tile_pool(name="work", bufs=GROUPS + 1) as work,
        tc.psum_pool(name="psum_t", bufs=2) as psum_t,
        tc.psum_pool(name="psum_b", bufs=1) as psum_b,
        tc.psum_pool(name="psum_acc", bufs=5) as psum_acc,
        tc.manual_schedule(),
    ):
        x_tiles = {}

        def load_features(i, queue):
            x = feat.tile([P, 2, K_PASS], BF16, name="x")
            queue.dma_start(out=x[:], in_=features[i])
            x_tiles[i] = x

        biases = {}

        bias_rows = keep.tile([P, 2, N_OUT], BF16)
        nc.vector.memset(bias_rows[:].bitcast(I32), 0)
        nc.scalar.dma_start(out=bias_rows[0:1, 0, :], in_=b_bbbb.unsqueeze(0))
        nc.scalar.dma_start(out=bias_rows[0:1, 1, :], in_=b_rfbb.unsqueeze(0))
        ones = keep.tile([P, P], BF16)
        nc.vector.memset(ones[:], 1.0)
        for i in LOAD_ORDER:
            load_features(i, nc.sync)
        bb_codes, bb_plane = load_weight(nc, keep, W_bbbb_words, W_bbbb_scales, "w_bb")
        rf_codes, rf_plane = load_weight(nc, keep, W_rfbb_words, W_rfbb_scales, "w_rf")

        identity = keep.tile([P, P], F32)
        make_identity(nc, identity[:])
        zero_column = keep.tile([P, 1], F32)
        nc.vector.memset(zero_column[:], 0.0)
        first_table = keep.tile([P, 1], F32)
        nc.scalar.activation(out=first_table[:], in_=zero_column[:], func=ACT.Sigmoid)

        transposed_tiles = {}
        grouped_tiles = {}
        x_codes = {}
        x_planes = {}
        products = {}
        v_tiles = {}
        q_tiles = {}

        def transpose(i):
            x_words = x_tiles[i][:].bitcast(F32)
            transposed = psum_t.tile([P, 2, 2, P], F32, name="transposed")
            for s in range(2):
                for u in range(2):
                    nc.tensor.transpose(transposed[:, s, u, :], x_words[:, s, u:WORDS:2], identity[:])
            transposed_tiles[i] = transposed

        def regroup(i):
            grouped = feat.tile([P, 2 * P * 4], BF16, align_bytes=64, name="grouped")
            nc.scalar.copy(
                out=grouped[:].bitcast(F32).rearrange("p (s b u) -> p s b u", s=2, u=2),
                in_=transposed_tiles[i][:].rearrange("p s u b -> p s b u"),
            )
            grouped_tiles[i] = grouped

        def quantise(i):
            codes = feat.tile([P, 2 * P], U32, align_bytes=64, name="codes")
            plane = feat.tile([P, 2 * P], U8, align_bytes=64, name="plane")
            nc.vector.quantize_mx(out=codes[:].bitcast(FP8X4), scales=plane[:], in_=grouped_tiles[i][:])
            x_codes[i] = codes
            x_planes[i] = plane

        def mx_pass(acc, pass_index, w_codes, w_plane, start, stop):
            tile_index, half = divmod(pass_index, 2)
            samples = slice(half * P, (half + 1) * P)
            nc.tensor.matmul_mx(
                out=acc[:],
                lhsT=x_codes[tile_index][:, samples].bitcast(FP8X4),
                lhsT_scale=x_planes[tile_index][:, samples],
                rhs=w_codes.bitcast(FP4X4),
                rhs_scale=w_plane,
                start=start,
                stop=stop,
            )

        def multiply(i):
            acc = psum_acc.tile([P, N_OUT], F32, name="acc")
            if i == RF:
                for s in range(2):
                    mx_pass(acc, GROUPS + s, rf_codes[:, s, :], rf_plane[:, s, :], s == 0, s == 1)
            else:
                mx_pass(acc, i, bb_codes[:, 0, :], bb_plane[:, 0, :], True, True)
            products[i] = acc

        bias_banks = {}

        def spread_bias(i):
            if "both" not in bias_banks:
                bank = psum_b.tile([P, 2, N_OUT], BF16, name="bias_bank")
                bias_banks["both"] = bank
            nc.tensor.matmul(out=bias_banks["both"][:, i, :], lhsT=ones[:], rhs=bias_rows[:, i, :], start=True, stop=True)

        def keep_bias(i):
            bias = keep.tile([P, N_OUT], BF16, name="bias%d" % i)
            nc.scalar.copy(out=bias[:], in_=bias_banks["both"][:, i, :])
            biases[i] = bias

        def add_bias(i):
            v = work.tile([P, N_OUT], F32, name="v")
            nc.vector.tensor_tensor(out=v[:], in0=products[i][:], in1=biases[i // GROUPS][:], op=ALU.add)
            v_tiles[i] = v

        def sigmoid(i):
            q = work.tile([P, N_OUT], F32, name="q")
            nc.scalar.activation(out=q[:], in_=v_tiles[i][:], func=ACT.Sigmoid, scale=-1.0)
            q_tiles[i] = q

        steps = {"T": transpose, "C": regroup, "Q": quantise, "M": multiply, "A": add_bias, "G": sigmoid, "B": spread_bias, "K": keep_bias}

        engines = {"v": nc.vector, "s": nc.scalar, "g": nc.gpsimd}
        w_tiles = {}
        d_tiles = {}
        roots = {}
        ratios = {}
        mishes = {}

        def square_q(e, i):
            w = work.tile([P, N_OUT], F32, name="w")
            if e == "s":
                nc.scalar.activation(out=w[:], in_=q_tiles[i][:], func=ACT.Square)
            else:
                engines[e].tensor_tensor(out=w[:], in0=q_tiles[i][:], in1=q_tiles[i][:], op=ALU.mult)
            w_tiles[i] = w

        def square_ahead(e, i):
            d = work.tile([P, N_OUT], F32, name="d")
            nc.vector.scalar_tensor_tensor(
                out=d[:], in0=w_tiles[i][:], scalar=2.0, in1=w_tiles[i][:], op0=ALU.add, op1=ALU.mult
            )
            d_tiles[i] = d

        def take_root(e, i):
            if i in d_tiles:
                ratio = work.tile([P, N_OUT], F32, name="ratio")
                nc.scalar.activation(
                    out=ratio[:], in_=d_tiles[i][:], func=ACT.Abs_reciprocal_sqrt, scale=0.25, bias=0.25
                )
                ratios[i] = ratio
            else:
                root = work.tile([P, N_OUT], F32, name="root")
                nc.scalar.activation(
                    out=root[:], in_=w_tiles[i][:], func=ACT.Abs_reciprocal_sqrt, scale=0.5, bias=0.5
                )
                roots[i] = root

        def square_root(e, i):
            ratio = work.tile([P, N_OUT], F32, name="ratio")
            if e == "s":
                nc.scalar.activation(out=ratio[:], in_=roots[i][:], func=ACT.Square)
            else:
                engines[e].tensor_tensor(out=ratio[:], in0=roots[i][:], in1=roots[i][:], op=ALU.mult)
            ratios[i] = ratio

        def multiply_v(e, i):
            mish = work.tile([P, N_OUT], F32, name="mish")
            nc.vector.scalar_tensor_tensor(
                out=mish[:], in0=ratios[i][:], scalar=-1.0, in1=v_tiles[i][:], op0=ALU.add, op1=ALU.mult
            )
            mishes[i] = mish

        def sum_and_store(e, g):
            total = work.tile([P, N_OUT], F32, name="total")
            engines[e].tensor_tensor(out=total[:], in0=mishes[g][:], in1=mishes[RF][:], op=ALU.add)
            nc.sync.dma_start(out=out[:, g, :], in_=total[:])

        def sum_and_store_halves(e, g):
            total = work.tile([P, N_OUT], F32, name="total")
            for half, queue in enumerate((nc.sync, nc.scalar)):
                cols = slice(half * (N_OUT // 2), (half + 1) * (N_OUT // 2))
                engines[e].tensor_tensor(out=total[:, cols], in0=mishes[g][:, cols], in1=mishes[RF][:, cols], op=ALU.add)
                queue.dma_start(out=out[:, g, cols], in_=total[:, cols])

        steps2 = {"Z": sum_and_store_halves, "W": square_q, "P": square_ahead, "R": take_root, "S": square_root, "X": multiply_v, "Y": sum_and_store}
        for word in (FIRST_HALF + " " + SECOND_HALF).split():
            if len(word) == 2:
                steps[word[0]](int(word[1]))
            else:
                steps2[word[0]](word[1], int(word[2]))
